import numpy as np
import ml_dtypes


def mxq(x, axis, fmt="e4m3"):
    dtype, down = {"e4m3": (ml_dtypes.float8_e4m3fn, 7), "e5m2": (ml_dtypes.float8_e5m2, 14)}[fmt]
    v = np.moveaxis(np.asarray(x, np.float32).astype(ml_dtypes.bfloat16).astype(np.float64), axis, -1)
    blocks = v.reshape(v.shape[:-1] + (-1, 32))
    amax = np.abs(blocks).max(-1, keepdims=True)
    byte = np.maximum(np.where(amax > 0, np.frexp(amax)[1] - 1 + 127, 0) - down, 1)
    scale = np.exp2(byte - 127.0)
    codes = (blocks / scale).astype(np.float32).astype(dtype).astype(np.float64)
    return np.moveaxis((codes * scale).reshape(v.shape), -1, axis)


WIDE = False


def mx_kscale(k):
    if not WIDE:
        return np.ones(k)
    levels = np.array([10, -10, 5, -5, 0])
    if k % 512:
        return np.exp2(np.random.permutation(np.resize(levels, k // 32))).repeat(32)
    a = np.empty((k // 512, 16))
    for p in range(k // 512):
        a[p, :8] = np.random.permutation(np.resize(levels, 8))
        for g in range(8):
            far = levels[np.abs(levels - a[p, g]) >= 10]
            a[p, g + 8] = far[np.random.randint(len(far))]
    return np.exp2(a.ravel()).repeat(32)


BF16 = ml_dtypes.bfloat16


def bf(x):
    return np.asarray(x, np.float32).astype(BF16)


def f64(x):
    return np.asarray(x).astype(np.float64)


M, K, N = 8192, 512, 512
BITS = 8


def setup_inputs():
    s = mx_kscale(K)
    return {"x": bf(np.random.standard_normal((M, K)) * s),
            "qw": bf(np.random.randint(0, 2 ** BITS, (N, K)) / s),
            "scale": bf(np.random.uniform(0.01, 0.02, 1) / np.sqrt(K)),
            "zero_point": bf(np.random.uniform(0.375, 0.625, 1) * 2 ** BITS / s.max()),
            "bias": bf(np.random.standard_normal(N))}


def reference(x, qw, scale, zero_point, bias):
    w = (f64(qw) - f64(zero_point)) * f64(scale)
    return (mxq(f64(x), 1, "e4m3") @ mxq(w, 1, "e4m3").T) + f64(bias)

@@ -1,0 +1,190 @@
+from contextlib import ExitStack
+
+import concourse.mybir as mybir
+from concourse.masks import make_identity
+
+F32 = mybir.dt.float32
+BF16 = mybir.dt.bfloat16
+U32 = mybir.dt.uint32
+U8 = mybir.dt.uint8
+FP8X4 = mybir.dt.float8_e4m3fn_x4
+ALU = mybir.AluOpType
+
+P = 128
+M, K, N = 8192, 512, 512
+FLOPS = 2 * M * K * N
+TILES = M // P
+GROUP = 4
+ROUNDS = TILES // GROUP
+AHEAD = 2
+X_CHUNKS = [4, 4, 8, 16, 32]
+STORE_TILES = [8, 8, 8, 8, 8, 8, 8, 4, 2, 1, 1]
+SCALAR_BANKS = (3,)
+KW = K // 2
+
+
+def tile_quantizedlinear_t_kernel(tc, x, qw, scale, zero_point, bias, out):
+    nc = tc.nc
+    x2 = x.rearrange("(p t) k -> p (t k)", t=TILES)
+    out2 = out.rearrange("(p t) n -> p (t n)", t=TILES)
+    with ExitStack() as ctx:
+        ctx.enter_context(tc.manual_schedule())
+        keep = ctx.enter_context(tc.tile_pool(name="keep", bufs=1))
+        gpool = ctx.enter_context(tc.tile_pool(name="gpool", bufs=3))
+        cpool = ctx.enter_context(tc.tile_pool(name="cpool", bufs=3))
+        opool = ctx.enter_context(tc.tile_pool(name="opool", bufs=7))
+        ps_t = ctx.enter_context(tc.psum_pool(name="ps_t", bufs=4))
+        ps_o = ctx.enter_context(tc.psum_pool(name="ps_o", bufs=4))
+
+        srow = keep.tile([P, 64], BF16, name="srow")
+        nc.gpsimd.memset(srow[:], 0.0)
+        brow = keep.tile([P, N], BF16, name="brow")
+        nc.vector.memset(brow[:], 0.0)
+        ones = keep.tile([P, P], BF16, name="ones")
+        nc.vector.memset(ones[:], 1.0)
+        ident = keep.tile([P, P], F32, name="ident")
+        make_identity(nc, ident[:])
+
+        q_sb = keep.tile([P, 4 * K], BF16, name="q_sb")
+        nc.sync.dma_start(
+            out=q_sb[:].rearrange("p (j k) -> p j k", j=4),
+            in_=qw.rearrange("(j p) k -> p j k", p=P),
+        )
+        nc.sync.dma_start(out=srow[0:1, 0:1], in_=scale.unsqueeze(0))
+        nc.sync.dma_start(out=srow[0:1, 32:33], in_=zero_point.unsqueeze(0))
+        x_words = []
+        t0 = 0
+        for ci, cnt in enumerate(X_CHUNKS):
+            x_sb = keep.tile([P, cnt * K], BF16, name="x_sb%d" % ci)
+            nc.sync.dma_start(out=x_sb[:], in_=x2[:, t0 * K : (t0 + cnt) * K])
+            if ci == 0:
+                nc.sync.dma_start(out=brow[0:1, :], in_=bias.unsqueeze(0))
+            xw = x_sb[:].bitcast(F32)
+            for i in range(cnt):
+                x_words.append(xw[:, i * KW : (i + 1) * KW])
+            t0 += cnt
+
+        sz_ps = ps_o.tile([P, 64], F32, name="sz_ps", tag="acc")
+        nc.tensor.matmul(sz_ps[:], lhsT=ones[:], rhs=srow[:], start=True, stop=True)
+        sz = keep.tile([P, 64], F32, name="sz")
+        nc.vector.tensor_copy(out=sz[:], in_=sz_ps[:])
+
+        q_words = q_sb[:].bitcast(F32)
+        w_grp = keep.tile([P, 4 * N], BF16, name="w_grp", align_bytes=64)
+        for h in range(2):
+            wt = ps_t.tile([P, 512], F32, name="wt", tag="tp")
+            for j in range(2):
+                for u in range(2):
+                    c0 = (2 * h + j) * KW
+                    nc.tensor.transpose(
+                        wt[:, u * 256 + j * P : u * 256 + (j + 1) * P],
+                        q_words[:, c0 + u : c0 + KW : 2],
+                        ident[:],
+                    )
+            nc.vector.tensor_scalar(
+                out=w_grp[:, h * 1024 : (h + 1) * 1024].rearrange(
+                    "p (n u e) -> p n u e", u=2, e=2
+                ),
+                in0=wt[:].bitcast(BF16).rearrange("p (u n e) -> p n u e", u=2, e=2),
+                scalar1=sz[:, 32:33],
+                scalar2=sz[:, 0:1],
+                op0=ALU.subtract,
+                op1=ALU.mult,
+            )
+        w_codes = keep.tile([P, N], U32, name="w_codes", align_bytes=64)
+        w_scales = keep.tile([P, N], U8, name="w_scales", align_bytes=64)
+        nc.vector.quantize_mx(
+            out=w_codes[:].bitcast(FP8X4), scales=w_scales[:], in_=w_grp[:]
+        )
+
+        b_ps = ps_o.tile([P, N], F32, name="b_ps", tag="acc")
+        nc.tensor.matmul(b_ps[:], lhsT=ones[:], rhs=brow[:], start=True, stop=True)
+        bias_sb = keep.tile([P, N], F32, name="bias_sb")
+        nc.scalar.copy(out=bias_sb[:], in_=b_ps[:])
+
+        grouped = {}
+        codes = {}
+
+        def transposes(g):
+            grp = gpool.tile([P, GROUP * K], BF16, name="grp", align_bytes=64)
+            grouped[g] = grp
+            grp_w = grp[:].bitcast(F32)
+            for h in range(GROUP // 2):
+                xt = ps_t.tile([P, 512], F32, name="xt", tag="tp")
+                for j in range(2):
+                    xw = x_words[g * GROUP + 2 * h + j]
+                    for u in range(2):
+                        nc.tensor.transpose(
+                            xt[:, u * 256 + j * P : u * 256 + (j + 1) * P],
+                            xw[:, u::2],
+                            ident[:],
+                        )
+                nc.scalar.copy(
+                    out=grp_w[:, h * 512 : (h + 1) * 512].rearrange(
+                        "p (r u) -> p r u", u=2
+                    ),
+                    in_=xt[:].rearrange("p (u r) -> p r u", u=2),
+                )
+
+        def quantise(g):
+            cw = cpool.tile([P, GROUP * P], U32, name="cw", align_bytes=64)
+            cs = cpool.tile([P, GROUP * P], U8, name="cs", align_bytes=64)
+            codes[g] = (cw, cs)
+            nc.vector.quantize_mx(
+                out=cw[:].bitcast(FP8X4), scales=cs[:], in_=grouped[g][:]
+            )
+
+        for g in range(AHEAD):
+            transposes(g)
+        quantise(0)
+
+        store_i = 0
+        store_first = 0
+        store_cnt = 0
+        o_sb = None
+        for g in range(ROUNDS):
+            if g + AHEAD < ROUNDS:
+                transposes(g + AHEAD)
+            cw, cs = codes[g]
+            accs = []
+            for j in range(GROUP):
+                acc = ps_o.tile([P, N], F32, name="acc", tag="acc")
+                accs.append(acc)
+                nc.tensor.matmul_mx(
+                    out=acc[:],
+                    lhsT=cw[:, j * P : (j + 1) * P].bitcast(FP8X4),
+                    lhsT_scale=cs[:, j * P : (j + 1) * P],
+                    rhs=w_codes[:].bitcast(FP8X4),
+                    rhs_scale=w_scales[:],
+                    start=True,
+                    stop=True,
+                )
+            if g + 1 < ROUNDS:
+                quantise(g + 1)
+            for j in range(GROUP):
+                t = g * GROUP + j
+                if t == store_first:
+                    store_cnt = STORE_TILES[store_i]
+                    o_sb = opool.tile([P, store_cnt * N], F32, name="o_sb")
+                c0 = (t - store_first) * N
+                if j in SCALAR_BANKS and g < ROUNDS - 1:
+                    nc.scalar.copy(out=o_sb[:, c0 : c0 + N], in_=accs[j][:])
+                    nc.gpsimd.tensor_tensor(
+                        out=o_sb[:, c0 : c0 + N],
+                        in0=o_sb[:, c0 : c0 + N],
+                        in1=bias_sb[:],
+                        op=ALU.add,
+                    )
+                else:
+                    nc.vector.tensor_tensor(
+                        out=o_sb[:, c0 : c0 + N],
+                        in0=accs[j][:],
+                        in1=bias_sb[:],
+                        op=ALU.add,
+                    )
+                if t == store_first + store_cnt - 1:
+                    nc.sync.dma_start(
+                        out=out2[:, store_first * N : (t + 1) * N], in_=o_sb[:]
+                    )
+                    store_first = t + 1
+                    store_i += 1

@@ -19,7 +19,7 @@ ROUNDS = TILES // GROUP
 AHEAD = 2
 X_CHUNKS = [4, 4, 8, 16, 32]
 STORE_TILES = [8, 8, 8, 8, 8, 8, 8, 4, 2, 1, 1]
-SCALAR_BANKS = (3,)
+SCALAR_BANKS = (0,)
 KW = K // 2
 
 

@@ -18,7 +18,7 @@ GROUP = 4
 ROUNDS = TILES // GROUP
 AHEAD = 2
 X_CHUNKS = [4, 4, 8, 16, 32]
-STORE_TILES = [8, 8, 8, 8, 8, 8, 8, 4, 2, 1, 1]
+STORE_TILES = [8, 8, 12, 12, 12, 12]
 SCALAR_BANKS = (0,)
 KW = K // 2
 
@@ -32,75 +32,70 @@ def tile_quantizedlinear_t_kernel(tc, x, qw, scale, zero_point, bias, out):
         keep = ctx.enter_context(tc.tile_pool(name="keep", bufs=1))
         gpool = ctx.enter_context(tc.tile_pool(name="gpool", bufs=3))
         cpool = ctx.enter_context(tc.tile_pool(name="cpool", bufs=3))
-        opool = ctx.enter_context(tc.tile_pool(name="opool", bufs=7))
+        opool = ctx.enter_context(tc.tile_pool(name="opool", bufs=1))
         ps_t = ctx.enter_context(tc.psum_pool(name="ps_t", bufs=4))
         ps_o = ctx.enter_context(tc.psum_pool(name="ps_o", bufs=4))
 
+        q_sb = keep.tile([P, 4 * K], BF16, name="q_sb")
+        nc.sync.dma_start(out=q_sb[:], in_=qw.rearrange("(p j) k -> p (j k)", j=4))
+        x_words = []
+        t0 = 0
+        for ci, cnt in enumerate(X_CHUNKS):
+            x_sb = keep.tile([P, cnt * K], BF16, name="x_sb%d" % ci)
+            nc.sync.dma_start(out=x_sb[:], in_=x2[:, t0 * K : (t0 + cnt) * K])
+            xw = x_sb[:].bitcast(F32)
+            for i in range(cnt):
+                x_words.append(xw[:, i * KW : (i + 1) * KW])
+            t0 += cnt
+
         srow = keep.tile([P, 64], BF16, name="srow")
-        nc.gpsimd.memset(srow[:], 0.0)
+        nc.vector.memset(srow[:], 0.0)
         brow = keep.tile([P, N], BF16, name="brow")
         nc.vector.memset(brow[:], 0.0)
         ones = keep.tile([P, P], BF16, name="ones")
         nc.vector.memset(ones[:], 1.0)
         ident = keep.tile([P, P], F32, name="ident")
         make_identity(nc, ident[:])
-
-        q_sb = keep.tile([P, 4 * K], BF16, name="q_sb")
-        nc.sync.dma_start(
-            out=q_sb[:].rearrange("p (j k) -> p j k", j=4),
-            in_=qw.rearrange("(j p) k -> p j k", p=P),
-        )
-        nc.sync.dma_start(out=srow[0:1, 0:1], in_=scale.unsqueeze(0))
-        nc.sync.dma_start(out=srow[0:1, 32:33], in_=zero_point.unsqueeze(0))
-        x_words = []
-        t0 = 0
-        for ci, cnt in enumerate(X_CHUNKS):
-            x_sb = keep.tile([P, cnt * K], BF16, name="x_sb%d" % ci)
-            nc.sync.dma_start(out=x_sb[:], in_=x2[:, t0 * K : (t0 + cnt) * K])
-            if ci == 0:
-                nc.sync.dma_start(out=brow[0:1, :], in_=bias.unsqueeze(0))
-            xw = x_sb[:].bitcast(F32)
-            for i in range(cnt):
-                x_words.append(xw[:, i * KW : (i + 1) * KW])
-            t0 += cnt
+        nc.scalar.dma_start(out=srow[0:1, 0:1], in_=scale.unsqueeze(0))
+        nc.scalar.dma_start(out=srow[0:1, 32:33], in_=zero_point.unsqueeze(0))
+        nc.scalar.dma_start(out=brow[0:1, :], in_=bias.unsqueeze(0))
 
         sz_ps = ps_o.tile([P, 64], F32, name="sz_ps", tag="acc")
         nc.tensor.matmul(sz_ps[:], lhsT=ones[:], rhs=srow[:], start=True, stop=True)
         sz = keep.tile([P, 64], F32, name="sz")
         nc.vector.tensor_copy(out=sz[:], in_=sz_ps[:])
 
-        q_words = q_sb[:].bitcast(F32)
+        w_sb = keep.tile([P, 4 * K], BF16, name="w_sb")
+        nc.vector.tensor_scalar(
+            out=w_sb[:],
+            in0=q_sb[:],
+            scalar1=sz[:, 32:33],
+            scalar2=sz[:, 0:1],
+            op0=ALU.subtract,
+            op1=ALU.mult,
+        )
+        w_words = w_sb[:].bitcast(F32)
         w_grp = keep.tile([P, 4 * N], BF16, name="w_grp", align_bytes=64)
+        w_grp_w = w_grp[:].bitcast(F32).rearrange("q (p h j u) -> q h p j u", h=2, j=2, u=2)
         for h in range(2):
             wt = ps_t.tile([P, 512], F32, name="wt", tag="tp")
             for j in range(2):
                 for u in range(2):
                     c0 = (2 * h + j) * KW
+                    b0 = (2 * j + u) * P
                     nc.tensor.transpose(
-                        wt[:, u * 256 + j * P : u * 256 + (j + 1) * P],
-                        q_words[:, c0 + u : c0 + KW : 2],
-                        ident[:],
+                        wt[:, b0 : b0 + P], w_words[:, c0 + u : c0 + KW : 2], ident[:]
                     )
-            nc.vector.tensor_scalar(
-                out=w_grp[:, h * 1024 : (h + 1) * 1024].rearrange(
-                    "p (n u e) -> p n u e", u=2, e=2
-                ),
-                in0=wt[:].bitcast(BF16).rearrange("p (u n e) -> p n u e", u=2, e=2),
-                scalar1=sz[:, 32:33],
-                scalar2=sz[:, 0:1],
-                op0=ALU.subtract,
-                op1=ALU.mult,
-            )
+            wt_v = wt[:].rearrange("q (j u p) -> q p j u", j=2, u=2)
+            if h == 0:
+                nc.scalar.copy(out=w_grp_w[:, h], in_=wt_v)
+            else:
+                nc.vector.tensor_copy(out=w_grp_w[:, h], in_=wt_v)
         w_codes = keep.tile([P, N], U32, name="w_codes", align_bytes=64)
         w_scales = keep.tile([P, N], U8, name="w_scales", align_bytes=64)
         nc.vector.quantize_mx(
             out=w_codes[:].bitcast(FP8X4), scales=w_scales[:], in_=w_grp[:]
         )
-
-        b_ps = ps_o.tile([P, N], F32, name="b_ps", tag="acc")
-        nc.tensor.matmul(b_ps[:], lhsT=ones[:], rhs=brow[:], start=True, stop=True)
-        bias_sb = keep.tile([P, N], F32, name="bias_sb")
-        nc.scalar.copy(out=bias_sb[:], in_=b_ps[:])
 
         grouped = {}
         codes = {}
@@ -134,17 +129,22 @@ def tile_quantizedlinear_t_kernel(tc, x, qw, scale, zero_point, bias, out):
                 out=cw[:].bitcast(FP8X4), scales=cs[:], in_=grouped[g][:]
             )
 
-        for g in range(AHEAD):
-            transposes(g)
+        transposes(0)
         quantise(0)
+
+        b_ps = ps_o.tile([P, N], F32, name="b_ps", tag="acc")
+        nc.tensor.matmul(b_ps[:], lhsT=ones[:], rhs=brow[:], start=True, stop=True)
+        bias_sb = keep.tile([P, N], F32, name="bias_sb")
+        nc.scalar.copy(out=bias_sb[:], in_=b_ps[:])
+
+        for g in range(1, AHEAD):
+            transposes(g)
 
         store_i = 0
         store_first = 0
         store_cnt = 0
         o_sb = None
         for g in range(ROUNDS):
-            if g + AHEAD < ROUNDS:
-                transposes(g + AHEAD)
             cw, cs = codes[g]
             accs = []
             for j in range(GROUP):
@@ -165,7 +165,7 @@ def tile_quantizedlinear_t_kernel(tc, x, qw, scale, zero_point, bias, out):
                 t = g * GROUP + j
                 if t == store_first:
                     store_cnt = STORE_TILES[store_i]
-                    o_sb = opool.tile([P, store_cnt * N], F32, name="o_sb")
+                    o_sb = opool.tile([P, store_cnt * N], F32, name="o_sb%d" % store_i)
                 c0 = (t - store_first) * N
                 if j in SCALAR_BANKS and g < ROUNDS - 1:
                     nc.scalar.copy(out=o_sb[:, c0 : c0 + N], in_=accs[j][:])
@@ -188,3 +188,5 @@ def tile_quantizedlinear_t_kernel(tc, x, qw, scale, zero_point, bias, out):
                     )
                     store_first = t + 1
                     store_i += 1
+            if g + AHEAD < ROUNDS:
+                transposes(g + AHEAD)

@@ -36,18 +36,6 @@ def tile_quantizedlinear_t_kernel(tc, x, qw, scale, zero_point, bias, out):
         ps_t = ctx.enter_context(tc.psum_pool(name="ps_t", bufs=4))
         ps_o = ctx.enter_context(tc.psum_pool(name="ps_o", bufs=4))
 
-        q_sb = keep.tile([P, 4 * K], BF16, name="q_sb")
-        nc.sync.dma_start(out=q_sb[:], in_=qw.rearrange("(p j) k -> p (j k)", j=4))
-        x_words = []
-        t0 = 0
-        for ci, cnt in enumerate(X_CHUNKS):
-            x_sb = keep.tile([P, cnt * K], BF16, name="x_sb%d" % ci)
-            nc.sync.dma_start(out=x_sb[:], in_=x2[:, t0 * K : (t0 + cnt) * K])
-            xw = x_sb[:].bitcast(F32)
-            for i in range(cnt):
-                x_words.append(xw[:, i * KW : (i + 1) * KW])
-            t0 += cnt
-
         srow = keep.tile([P, 64], BF16, name="srow")
         nc.vector.memset(srow[:], 0.0)
         brow = keep.tile([P, N], BF16, name="brow")
@@ -56,9 +44,22 @@ def tile_quantizedlinear_t_kernel(tc, x, qw, scale, zero_point, bias, out):
         nc.vector.memset(ones[:], 1.0)
         ident = keep.tile([P, P], F32, name="ident")
         make_identity(nc, ident[:])
-        nc.scalar.dma_start(out=srow[0:1, 0:1], in_=scale.unsqueeze(0))
-        nc.scalar.dma_start(out=srow[0:1, 32:33], in_=zero_point.unsqueeze(0))
-        nc.scalar.dma_start(out=brow[0:1, :], in_=bias.unsqueeze(0))
+
+        q_sb = keep.tile([P, 4 * K], BF16, name="q_sb")
+        nc.sync.dma_start(out=q_sb[:], in_=qw.rearrange("(p j) k -> p (j k)", j=4))
+        nc.sync.dma_start(out=srow[0:1, 0:1], in_=scale.unsqueeze(0))
+        nc.sync.dma_start(out=srow[0:1, 32:33], in_=zero_point.unsqueeze(0))
+        x_words = []
+        t0 = 0
+        for ci, cnt in enumerate(X_CHUNKS):
+            x_sb = keep.tile([P, cnt * K], BF16, name="x_sb%d" % ci)
+            nc.sync.dma_start(out=x_sb[:], in_=x2[:, t0 * K : (t0 + cnt) * K])
+            if ci == 0:
+                nc.sync.dma_start(out=brow[0:1, :], in_=bias.unsqueeze(0))
+            xw = x_sb[:].bitcast(F32)
+            for i in range(cnt):
+                x_words.append(xw[:, i * KW : (i + 1) * KW])
+            t0 += cnt
 
         sz_ps = ps_o.tile([P, 64], F32, name="sz_ps", tag="acc")
         nc.tensor.matmul(sz_ps[:], lhsT=ones[:], rhs=srow[:], start=True, stop=True)

@@ -18,7 +18,7 @@ GROUP = 4
 ROUNDS = TILES // GROUP
 AHEAD = 2
 X_CHUNKS = [4, 4, 8, 16, 32]
-STORE_TILES = [8, 8, 12, 12, 12, 12]
+STORE_TILES = [8] * 8
 SCALAR_BANKS = (0,)
 KW = K // 2
 
@@ -66,18 +66,9 @@ def tile_quantizedlinear_t_kernel(tc, x, qw, scale, zero_point, bias, out):
         sz = keep.tile([P, 64], F32, name="sz")
         nc.vector.tensor_copy(out=sz[:], in_=sz_ps[:])
 
-        w_sb = keep.tile([P, 4 * K], BF16, name="w_sb")
-        nc.vector.tensor_scalar(
-            out=w_sb[:],
-            in0=q_sb[:],
-            scalar1=sz[:, 32:33],
-            scalar2=sz[:, 0:1],
-            op0=ALU.subtract,
-            op1=ALU.mult,
-        )
-        w_words = w_sb[:].bitcast(F32)
+        q_words = q_sb[:].bitcast(F32)
         w_grp = keep.tile([P, 4 * N], BF16, name="w_grp", align_bytes=64)
-        w_grp_w = w_grp[:].bitcast(F32).rearrange("q (p h j u) -> q h p j u", h=2, j=2, u=2)
+        w_grp_v = w_grp[:].rearrange("q (p h m e) -> q h p m e", h=2, m=4, e=2)
         for h in range(2):
             wt = ps_t.tile([P, 512], F32, name="wt", tag="tp")
             for j in range(2):
@@ -85,13 +76,16 @@ def tile_quantizedlinear_t_kernel(tc, x, qw, scale, zero_point, bias, out):
                     c0 = (2 * h + j) * KW
                     b0 = (2 * j + u) * P
                     nc.tensor.transpose(
-                        wt[:, b0 : b0 + P], w_words[:, c0 + u : c0 + KW : 2], ident[:]
+                        wt[:, b0 : b0 + P], q_words[:, c0 + u : c0 + KW : 2], ident[:]
                     )
-            wt_v = wt[:].rearrange("q (j u p) -> q p j u", j=2, u=2)
-            if h == 0:
-                nc.scalar.copy(out=w_grp_w[:, h], in_=wt_v)
-            else:
-                nc.vector.tensor_copy(out=w_grp_w[:, h], in_=wt_v)
+            nc.vector.tensor_scalar(
+                out=w_grp_v[:, h],
+                in0=wt[:].bitcast(BF16).rearrange("q (m p e) -> q p m e", m=4, e=2),
+                scalar1=sz[:, 32:33],
+                scalar2=sz[:, 0:1],
+                op0=ALU.subtract,
+                op1=ALU.mult,
+            )
         w_codes = keep.tile([P, N], U32, name="w_codes", align_bytes=64)
         w_scales = keep.tile([P, N], U8, name="w_scales", align_bytes=64)
         nc.vector.quantize_mx(
@@ -146,6 +140,8 @@ def tile_quantizedlinear_t_kernel(tc, x, qw, scale, zero_point, bias, out):
         store_cnt = 0
         o_sb = None
         for g in range(ROUNDS):
+            if 0 < g < ROUNDS - AHEAD:
+                transposes(g + AHEAD)
             cw, cs = codes[g]
             accs = []
             for j in range(GROUP):
@@ -189,5 +185,5 @@ def tile_quantizedlinear_t_kernel(tc, x, qw, scale, zero_point, bias, out):
                     )
                     store_first = t + 1
                     store_i += 1
-            if g + AHEAD < ROUNDS:
-                transposes(g + AHEAD)
+            if g == 0:
+                transposes(AHEAD)

from contextlib import ExitStack

import concourse.mybir as mybir
from concourse.masks import make_identity

F32 = mybir.dt.float32
BF16 = mybir.dt.bfloat16
U32 = mybir.dt.uint32
U8 = mybir.dt.uint8
FP8X4 = mybir.dt.float8_e4m3fn_x4
ALU = mybir.AluOpType

P = 128
M, K, N = 8192, 512, 512
FLOPS = 2 * M * K * N
TILES = M // P
GROUP = 4
ROUNDS = TILES // GROUP
AHEAD = 2
X_CHUNKS = [4, 4, 8, 16, 32]
STORE_TILES = [8] * 8
SCALAR_BANKS = (0,)
KW = K // 2


def tile_quantizedlinear_t_kernel(tc, x, qw, scale, zero_point, bias, out):
    nc = tc.nc
    x2 = x.rearrange("(p t) k -> p (t k)", t=TILES)
    out2 = out.rearrange("(p t) n -> p (t n)", t=TILES)
    with ExitStack() as ctx:
        ctx.enter_context(tc.manual_schedule())
        keep = ctx.enter_context(tc.tile_pool(name="keep", bufs=1))
        gpool = ctx.enter_context(tc.tile_pool(name="gpool", bufs=3))
        cpool = ctx.enter_context(tc.tile_pool(name="cpool", bufs=3))
        opool = ctx.enter_context(tc.tile_pool(name="opool", bufs=1))
        ps_t = ctx.enter_context(tc.psum_pool(name="ps_t", bufs=4))
        ps_o = ctx.enter_context(tc.psum_pool(name="ps_o", bufs=4))

        srow = keep.tile([P, 64], BF16, name="srow")
        nc.vector.memset(srow[:], 0.0)
        brow = keep.tile([P, N], BF16, name="brow")
        nc.vector.memset(brow[:], 0.0)
        ones = keep.tile([P, P], BF16, name="ones")
        nc.vector.memset(ones[:], 1.0)
        ident = keep.tile([P, P], F32, name="ident")
        make_identity(nc, ident[:])

        q_sb = keep.tile([P, 4 * K], BF16, name="q_sb")
        nc.sync.dma_start(out=q_sb[:], in_=qw.rearrange("(p j) k -> p (j k)", j=4))
        nc.sync.dma_start(out=srow[0:1, 0:1], in_=scale.unsqueeze(0))
        nc.sync.dma_start(out=srow[0:1, 32:33], in_=zero_point.unsqueeze(0))
        x_words = []
        t0 = 0
        for ci, cnt in enumerate(X_CHUNKS):
            x_sb = keep.tile([P, cnt * K], BF16, name="x_sb%d" % ci)
            nc.sync.dma_start(out=x_sb[:], in_=x2[:, t0 * K : (t0 + cnt) * K])
            if ci == 0:
                nc.sync.dma_start(out=brow[0:1, :], in_=bias.unsqueeze(0))
            xw = x_sb[:].bitcast(F32)
            for i in range(cnt):
                x_words.append(xw[:, i * KW : (i + 1) * KW])
            t0 += cnt

        sz_ps = ps_o.tile([P, 64], F32, name="sz_ps", tag="acc")
        nc.tensor.matmul(sz_ps[:], lhsT=ones[:], rhs=srow[:], start=True, stop=True)
        sz = keep.tile([P, 64], F32, name="sz")
        nc.vector.tensor_copy(out=sz[:], in_=sz_ps[:])

        q_words = q_sb[:].bitcast(F32)
        w_grp = keep.tile([P, 4 * N], BF16, name="w_grp", align_bytes=64)
        w_grp_v = w_grp[:].rearrange("q (p h m e) -> q h p m e", h=2, m=4, e=2)
        for h in range(2):
            wt = ps_t.tile([P, 512], F32, name="wt", tag="tp")
            for j in range(2):
                for u in range(2):
                    c0 = (2 * h + j) * KW
                    b0 = (2 * j + u) * P
                    nc.tensor.transpose(
                        wt[:, b0 : b0 + P], q_words[:, c0 + u : c0 + KW : 2], ident[:]
                    )
            nc.vector.tensor_scalar(
                out=w_grp_v[:, h],
                in0=wt[:].bitcast(BF16).rearrange("q (m p e) -> q p m e", m=4, e=2),
                scalar1=sz[:, 32:33],
                scalar2=sz[:, 0:1],
                op0=ALU.subtract,
                op1=ALU.mult,
            )
        w_codes = keep.tile([P, N], U32, name="w_codes", align_bytes=64)
        w_scales = keep.tile([P, N], U8, name="w_scales", align_bytes=64)
        nc.vector.quantize_mx(
            out=w_codes[:].bitcast(FP8X4), scales=w_scales[:], in_=w_grp[:]
        )

        grouped = {}
        codes = {}

        def transposes(g):
            grp = gpool.tile([P, GROUP * K], BF16, name="grp", align_bytes=64)
            grouped[g] = grp
            grp_w = grp[:].bitcast(F32)
            for h in range(GROUP // 2):
                xt = ps_t.tile([P, 512], F32, name="xt", tag="tp")
                for j in range(2):
                    xw = x_words[g * GROUP + 2 * h + j]
                    for u in range(2):
                        nc.tensor.transpose(
                            xt[:, u * 256 + j * P : u * 256 + (j + 1) * P],
                            xw[:, u::2],
                            ident[:],
                        )
                nc.scalar.copy(
                    out=grp_w[:, h * 512 : (h + 1) * 512].rearrange(
                        "p (r u) -> p r u", u=2
                    ),
                    in_=xt[:].rearrange("p (u r) -> p r u", u=2),
                )

        def quantise(g):
            cw = cpool.tile([P, GROUP * P], U32, name="cw", align_bytes=64)
            cs = cpool.tile([P, GROUP * P], U8, name="cs", align_bytes=64)
            codes[g] = (cw, cs)
            nc.vector.quantize_mx(
                out=cw[:].bitcast(FP8X4), scales=cs[:], in_=grouped[g][:]
            )

        transposes(0)
        quantise(0)

        b_ps = ps_o.tile([P, N], F32, name="b_ps", tag="acc")
        nc.tensor.matmul(b_ps[:], lhsT=ones[:], rhs=brow[:], start=True, stop=True)
        bias_sb = keep.tile([P, N], F32, name="bias_sb")
        nc.scalar.copy(out=bias_sb[:], in_=b_ps[:])

        for g in range(1, AHEAD):
            transposes(g)

        store_i = 0
        store_first = 0
        store_cnt = 0
        o_sb = None
        for g in range(ROUNDS):
            if 0 < g < ROUNDS - AHEAD:
                transposes(g + AHEAD)
            cw, cs = codes[g]
            accs = []
            for j in range(GROUP):
                acc = ps_o.tile([P, N], F32, name="acc", tag="acc")
                accs.append(acc)
                nc.tensor.matmul_mx(
                    out=acc[:],
                    lhsT=cw[:, j * P : (j + 1) * P].bitcast(FP8X4),
                    lhsT_scale=cs[:, j * P : (j + 1) * P],
                    rhs=w_codes[:].bitcast(FP8X4),
                    rhs_scale=w_scales[:],
                    start=True,
                    stop=True,
                )
            if g + 1 < ROUNDS:
                quantise(g + 1)
            for j in range(GROUP):
                t = g * GROUP + j
                if t == store_first:
                    store_cnt = STORE_TILES[store_i]
                    o_sb = opool.tile([P, store_cnt * N], F32, name="o_sb%d" % store_i)
                c0 = (t - store_first) * N
                if j in SCALAR_BANKS and g < ROUNDS - 1:
                    nc.scalar.copy(out=o_sb[:, c0 : c0 + N], in_=accs[j][:])
                    nc.gpsimd.tensor_tensor(
                        out=o_sb[:, c0 : c0 + N],
                        in0=o_sb[:, c0 : c0 + N],
                        in1=bias_sb[:],
                        op=ALU.add,
                    )
                else:
                    nc.vector.tensor_tensor(
                        out=o_sb[:, c0 : c0 + N],
                        in0=accs[j][:],
                        in1=bias_sb[:],
                        op=ALU.add,
                    )
                if t == store_first + store_cnt - 1:
                    nc.sync.dma_start(
                        out=out2[:, store_first * N : (t + 1) * N], in_=o_sb[:]
                    )
                    store_first = t + 1
                    store_i += 1
            if g == 0:
                transposes(AHEAD)
